import numpy as np
import ml_dtypes


def mxq(x, axis, fmt="e4m3"):
    dtype, down = {"e4m3": (ml_dtypes.float8_e4m3fn, 7), "e5m2": (ml_dtypes.float8_e5m2, 14)}[fmt]
    v = np.moveaxis(np.asarray(x, np.float32).astype(ml_dtypes.bfloat16).astype(np.float64), axis, -1)
    blocks = v.reshape(v.shape[:-1] + (-1, 32))
    amax = np.abs(blocks).max(-1, keepdims=True)
    byte = np.maximum(np.where(amax > 0, np.frexp(amax)[1] - 1 + 127, 0) - down, 1)
    scale = np.exp2(byte - 127.0)
    codes = (blocks / scale).astype(np.float32).astype(dtype).astype(np.float64)
    return np.moveaxis((codes * scale).reshape(v.shape), -1, axis)


WIDE = False


def mx_kscale(k):
    if not WIDE:
        return np.ones(k)
    levels = np.array([10, -10, 5, -5, 0])
    a = np.random.permutation(np.resize(levels, k // 512 * 4)).reshape(k // 512, 4)
    idx = np.arange(k)
    return np.exp2(a[idx // 512, idx % 128 // 32])


BF16 = ml_dtypes.bfloat16


def bf(x):
    return np.asarray(x, np.float32).astype(BF16)


def f64(x):
    return np.asarray(x).astype(np.float64)


B, CK, CV, NO, T, H, W = 16, 128, 256, 2, 2, 16, 16
N = T * H * W
P = H * W
C = NO * CV


def setup_inputs():
    s = mx_kscale(N)
    g = np.exp2(np.round(np.log2(np.mean(s))))
    mk = np.random.standard_normal((B, CK, N))
    qk = np.random.standard_normal((B, CK, P))
    qe = np.random.uniform(0.0, 1.0, (B, CK, P))
    ms = bf(0.75 + 0.5 * np.random.uniform(0.0, 1.0, (B, N)))
    d = (np.log2(np.max(s)) - np.log2(s))[None, :] * np.log(2.0) * np.sqrt(CK) / f64(ms)
    a0 = mk[:, 0, :] ** 2 + d
    mk[:, 0, :] = np.sqrt(a0)
    qk[:, 0, :] = 0.0
    qe[:, 0, :] = 1.0
    mk, qk, qe = bf(mk), bf(qk), bf(qe)
    mksq = f64(mk) * f64(mk)
    mksq[:, 0, :] = a0
    return {"memory_key": mk,
            "memory_key_sq": bf(mksq),
            "query_key": qk,
            "query_selection": qe,
            "query_key_sel": bf(f64(qk) * f64(qe)),
            "memory_shrinkage": ms,
            "memory_value": bf(np.random.standard_normal((B, C, N)) * g / s[None, None, :])}


def reference(memory_key, memory_key_sq, query_key, query_selection, query_key_sel, memory_shrinkage, memory_value):
    qe = f64(query_selection)
    qs = f64(query_key_sel)
    ms = f64(memory_shrinkage)[:, :, None]
    a_sq = f64(memory_key_sq).transpose(0, 2, 1) @ qe
    two_ab = 2.0 * (f64(memory_key).transpose(0, 2, 1) @ qs)
    b_sq = np.sum(qs * f64(query_key), axis=1, keepdims=True)
    similarity = (-a_sq + two_ab - b_sq) * ms * (1.0 / np.sqrt(CK))
    e = np.exp(similarity - similarity.max(axis=1, keepdims=True))
    affinity = e / e.sum(axis=1, keepdims=True)
    return mxq(f64(memory_value), 2, "e4m3") @ mxq(affinity, 1, "e4m3")

@@ -1,0 +1,314 @@
+import math
+from contextlib import ExitStack
+
+import concourse.mybir as mybir
+from concourse.masks import make_identity
+
+F32 = mybir.dt.float32
+BF16 = mybir.dt.bfloat16
+U32 = mybir.dt.uint32
+U8 = mybir.dt.uint8
+FP8X4 = mybir.dt.float8_e4m3fn_x4
+ALU = mybir.AluOpType
+ACT = mybir.ActivationFunctionType
+AXIS = mybir.AxisListType
+
+P = 128
+B = 16
+N = 512
+Q = 256
+C = 512
+Q_TILES = Q // P
+C_TILES = C // P
+PACK = 4
+INV_SQRT_CK = 1.0 / math.sqrt(128.0)
+VAL_LEAD = 1
+
+FLOPS = B * (2 * 2 * P * N * Q + 2 * C * N * Q)
+
+
+def tile_vidsam_pa_t_kernel(
+    tc,
+    memory_key,
+    memory_key_sq,
+    query_key,
+    query_selection,
+    query_key_sel,
+    memory_shrinkage,
+    memory_value,
+    out,
+):
+    nc = tc.nc
+    with ExitStack() as ctx:
+        consts = ctx.enter_context(tc.tile_pool(name="consts", bufs=1))
+        loads = ctx.enter_context(tc.tile_pool(name="loads", bufs=B))
+        work = ctx.enter_context(tc.tile_pool(name="work", bufs=2))
+        psum = ctx.enter_context(tc.psum_pool(name="psum", bufs=8))
+        ctx.enter_context(tc.manual_schedule())
+
+        ms_rows = consts.tile([P, N], BF16)
+        nc.vector.memset(ms_rows[:], 0.0)
+        nc.sync.dma_start(out=ms_rows[0:B, :], in_=memory_shrinkage)
+        qe_sb, ksq_sb, qs_sb, key_sb, qk_sb, val_sb = {}, {}, {}, {}, {}, {}
+        for b in range(B):
+            qs_sb[b] = loads.tile([P, Q], BF16, name="qs")
+            nc.sync.dma_start(out=qs_sb[b][:], in_=query_key_sel[b])
+            qk_sb[b] = loads.tile([P, Q], BF16, name="qk")
+            nc.sync.dma_start(out=qk_sb[b][:], in_=query_key[b])
+            qe_sb[b] = loads.tile([P, Q], BF16, name="qe")
+            nc.sync.dma_start(out=qe_sb[b][:], in_=query_selection[b])
+            ksq_sb[b] = loads.tile([P, N], BF16, name="ksq")
+            nc.sync.dma_start(out=ksq_sb[b][:], in_=memory_key_sq[b])
+            key_sb[b] = loads.tile([P, N], BF16, name="key")
+            nc.sync.dma_start(out=key_sb[b][:], in_=memory_key[b])
+            val_sb[b] = loads.tile([P, C_TILES * N], BF16, name="val")
+            nc.sync.dma_start(
+                out=val_sb[b][:],
+                in_=memory_value[b].rearrange("(r t) n -> r (t n)", t=C_TILES),
+            )
+
+        ident_bf = consts.tile([P, P], BF16)
+        make_identity(nc, ident_bf[:])
+        ident_f32 = consts.tile([P, P], F32)
+        make_identity(nc, ident_f32[:])
+        ones_f32 = consts.tile([P, 2], F32)
+        nc.vector.memset(ones_f32[:], 1.0)
+        warm = consts.tile([P, 1], F32)
+        nc.scalar.activation(out=warm[:], in_=ones_f32[:, 0:1], func=ACT.Exp)
+
+        ms_rows_ew = ms_rows[:].rearrange("r (w e) -> r e w", e=2)
+        ms_cols_ps = psum.tile([P, 4, P], BF16, tag="bank")
+        for e in range(2):
+            for u in range(2):
+                nc.tensor.transpose(
+                    ms_cols_ps[:, 2 * e + u, :],
+                    ms_rows_ew[:, e, u * P : (u + 1) * P],
+                    ident_bf[:],
+                )
+        ms_cols = consts.tile([P, 4, B], BF16)
+        nc.vector.tensor_copy(out=ms_cols[:], in_=ms_cols_ps[:, :, 0:B])
+
+        qs_m2, prod = {}, {}
+        spread_ps, shrink = {}, {}
+        bsq_ps, d_ps, dist, neg_max = {}, {}, {}, {}
+        expo, expo_sum = {}, {}
+        affinity, aff_flipped, aff_grouped, aff_codes, aff_scales = {}, {}, {}, {}, {}
+        val_grouped, val_codes, val_scales = {}, {}, {}
+        o_ps, result = {}, {}
+
+        def prepare_queries(b):
+            prod[b] = work.tile([P, Q], F32, name="prod", bufs=3)
+            nc.gpsimd.tensor_tensor(out=prod[b][:], in0=qs_sb[b][:], in1=qk_sb[b][:], op=ALU.mult)
+            qs_m2[b] = work.tile([P, Q], BF16, name="qs_m2", bufs=3)
+            nc.gpsimd.tensor_scalar(
+                out=qs_m2[b][:], in0=qs_sb[b][:], scalar1=-2.0, scalar2=0.0, op0=ALU.mult, op1=ALU.add
+            )
+
+        def spread_shrinkage(b):
+            spread_ps[b] = psum.tile([P, 2, N], BF16, tag="bank", name="spread_ps")
+            for j in range(2):
+                for k in range(4):
+                    nc.tensor.transpose(
+                        spread_ps[b][:, j, k * P : (k + 1) * P],
+                        ms_cols[:, k, b + j : b + j + 1].to_broadcast([P, P]),
+                        ident_bf[:],
+                    )
+
+        def copy_shrinkage(b):
+            spread = work.tile([P, 2, N], BF16)
+            nc.vector.tensor_copy(out=spread[:], in_=spread_ps[b][:])
+            shrink[b] = spread[:, 0, :]
+            shrink[b + 1] = spread[:, 1, :]
+
+        def distances(b):
+            bsq_ps[b] = psum.tile([P, Q_TILES, 2], F32, tag="bank", name="bsq_ps")
+            for i in range(Q_TILES):
+                nc.tensor.matmul(
+                    out=bsq_ps[b][:, i, :],
+                    lhsT=prod[b][:, i * P : (i + 1) * P],
+                    rhs=ones_f32[:],
+                    start=True,
+                    stop=True,
+                )
+            for i in range(Q_TILES):
+                q_cols = slice(i * P, (i + 1) * P)
+                d_ps[b, i] = psum.tile([P, 2, N // 2], F32, tag="bank", name="d_ps")
+                nc.tensor.matmul(
+                    out=d_ps[b, i][:],
+                    lhsT=qe_sb[b][:, q_cols],
+                    rhs=ksq_sb[b][:].rearrange("c (w e) -> c e w", e=2),
+                    start=True,
+                    stop=False,
+                )
+                nc.tensor.matmul(
+                    out=d_ps[b, i][:],
+                    lhsT=qs_m2[b][:, q_cols],
+                    rhs=key_sb[b][:].rearrange("c (w e) -> c e w", e=2),
+                    start=False,
+                    stop=True,
+                )
+
+        def scale_distances(b, i):
+            if i == 0:
+                dist[b] = work.tile([P, Q_TILES, N], F32, name="dist")
+            nc.vector.scalar_tensor_tensor(
+                out=dist[b][:, i, :],
+                in0=d_ps[b, i][:].rearrange("p e w -> p (e w)"),
+                scalar=bsq_ps[b][:, i, 0:1],
+                in1=shrink[b],
+                op0=ALU.add,
+                op1=ALU.mult,
+            )
+
+        def row_maximum(b):
+            dist_min = work.tile([P, Q_TILES], F32)
+            nc.vector.tensor_reduce(out=dist_min[:], in_=dist[b][:], axis=AXIS.X, op=ALU.min)
+            neg_max[b] = work.tile([P, Q_TILES], F32, name="neg_max")
+            nc.vector.tensor_scalar(
+                out=neg_max[b][:], in0=dist_min[:], scalar1=INV_SQRT_CK, scalar2=None, op0=ALU.mult
+            )
+
+        def exponentials(b):
+            expo[b] = work.tile([P, Q_TILES, N], F32, name="expo")
+            expo_sum[b] = work.tile([P, Q_TILES], F32, name="expo_sum")
+            for i in range(Q_TILES):
+                nc.scalar.activation(
+                    out=expo[b][:, i, :],
+                    in_=dist[b][:, i, :],
+                    func=ACT.Exp,
+                    bias=neg_max[b][:, i : i + 1],
+                    scale=-INV_SQRT_CK,
+                    accum_out=expo_sum[b][:, i : i + 1],
+                )
+
+        def normalise(b):
+            inv_sum = work.tile([P, Q_TILES], F32)
+            nc.vector.reciprocal(out=inv_sum[:], in_=expo_sum[b][:])
+            affinity[b] = work.tile([P, Q_TILES, N], BF16, name="affinity")
+            for i in range(Q_TILES):
+                nc.gpsimd.tensor_scalar(
+                    out=affinity[b][:, i, :],
+                    in0=expo[b][:, i, :],
+                    scalar1=inv_sum[:, i : i + 1],
+                    scalar2=0.0,
+                    op0=ALU.mult,
+                    op1=ALU.add,
+                )
+
+        def transpose_affinity(b):
+            aff_flipped[b] = psum.tile([P, PACK, Q], BF16, tag="bank", name="aff_flipped")
+            for i in range(Q_TILES):
+                for e in range(2):
+                    for u in range(2):
+                        first = (2 * e + u) * P
+                        nc.tensor.transpose(
+                            aff_flipped[b][:, 2 * u + e, i * P : (i + 1) * P],
+                            affinity[b][:, i, first : first + P],
+                            ident_bf[:],
+                        )
+
+        def group_affinity(b):
+            aff_grouped[b] = work.tile([P, Q, PACK], BF16, align_bytes=64, name="aff_grouped")
+            nc.scalar.copy(out=aff_grouped[b][:], in_=aff_flipped[b][:].rearrange("q k p -> q p k"))
+
+        def quantise_affinity(b):
+            aff_codes[b] = work.tile([P, Q], U32, align_bytes=64, name="aff_codes")
+            aff_scales[b] = work.tile([P, Q], U8, align_bytes=64, name="aff_scales")
+            nc.vector.quantize_mx(
+                out=aff_codes[b][:].bitcast(FP8X4),
+                scales=aff_scales[b][:],
+                in_=aff_grouped[b][:].rearrange("q p k -> q (p k)"),
+            )
+
+        def transpose_values(b):
+            val_words = val_sb[b][:].bitcast(F32)
+            val_grouped[b] = work.tile([P, C * PACK], BF16, align_bytes=64, name="val_grouped")
+            grouped_words = val_grouped[b][:].bitcast(F32)
+            for h in range(2):
+                flipped = psum.tile([P, 2, 2 * P], F32, tag="bank")
+                for tl in range(2):
+                    for u in range(2):
+                        first = (2 * h + tl) * (N // 2) + u * P
+                        nc.tensor.transpose(
+                            flipped[:, u, tl * P : (tl + 1) * P],
+                            val_words[:, first : first + P],
+                            ident_f32[:],
+                        )
+                nc.scalar.copy(
+                    out=grouped_words[:, h * N : (h + 1) * N].rearrange("q (c u) -> q c u", u=2),
+                    in_=flipped[:].rearrange("q u c -> q c u"),
+                )
+
+        def quantise_values(b):
+            val_codes[b] = work.tile([P, C], U32, align_bytes=64, name="val_codes", bufs=VAL_LEAD + 3)
+            val_scales[b] = work.tile([P, C], U8, align_bytes=64, name="val_scales", bufs=VAL_LEAD + 3)
+            nc.vector.quantize_mx(
+                out=val_codes[b][:].bitcast(FP8X4), scales=val_scales[b][:], in_=val_grouped[b][:]
+            )
+
+        def read_memory(b):
+            for h in range(2):
+                o_ps[b, h] = psum.tile([P, 2, Q], F32, tag="bank", name="o_ps")
+                for tl in range(2):
+                    c_cols = slice((2 * h + tl) * P, (2 * h + tl + 1) * P)
+                    nc.tensor.matmul_mx(
+                        out=o_ps[b, h][:, tl, :],
+                        lhsT=val_codes[b][:, c_cols].bitcast(FP8X4),
+                        lhsT_scale=val_scales[b][:, c_cols],
+                        rhs=aff_codes[b][:].bitcast(FP8X4),
+                        rhs_scale=aff_scales[b][:],
+                        start=True,
+                        stop=True,
+                    )
+
+        def copy_result(b):
+            result[b] = work.tile([P, C_TILES * Q], F32, name="result", bufs=3)
+            nc.scalar.copy(out=result[b][:, 0 : 2 * Q], in_=o_ps[b, 0][:].rearrange("r t p -> r (t p)"))
+            nc.vector.tensor_copy(
+                out=result[b][:, 2 * Q : 4 * Q], in_=o_ps[b, 1][:].rearrange("r t p -> r (t p)")
+            )
+
+        def store_result(b):
+            nc.scalar.dma_start(
+                out=out[b].rearrange("(r t) p -> r (t p)", t=C_TILES), in_=result[b][:]
+            )
+
+        def live(b):
+            return 0 <= b < B
+
+        prepare_queries(0)
+        for step in range(-VAL_LEAD, B + 2):
+            nxt, new, mid, old, val = step + 1, step, step - 1, step - 2, step + VAL_LEAD
+            if live(old):
+                group_affinity(old)
+            if live(val):
+                transpose_values(val)
+            if live(new):
+                scale_distances(new, 0)
+            if live(mid):
+                normalise(mid)
+            if live(new):
+                scale_distances(new, 1)
+            if live(nxt) and nxt % 2 == 0:
+                spread_shrinkage(nxt)
+            if live(old):
+                quantise_affinity(old)
+                read_memory(old)
+            if live(new):
+                row_maximum(new)
+            if live(old):
+                copy_result(old)
+            if live(nxt + 1):
+                prepare_queries(nxt + 1)
+            if live(nxt):
+                distances(nxt)
+            if live(mid):
+                transpose_affinity(mid)
+            if live(new):
+                exponentials(new)
+            if live(old):
+                store_result(old)
+            if live(val):
+                quantise_values(val)
+            if live(nxt) and nxt % 2 == 0:
+                copy_shrinkage(nxt)

@@ -22,7 +22,6 @@ Q_TILES = Q // P
 C_TILES = C // P
 PACK = 4
 INV_SQRT_CK = 1.0 / math.sqrt(128.0)
-VAL_LEAD = 1
 
 FLOPS = B * (2 * 2 * P * N * Q + 2 * C * N * Q)
 
@@ -91,7 +90,7 @@ def tile_vidsam_pa_t_kernel(
         qs_m2, prod = {}, {}
         spread_ps, shrink = {}, {}
         bsq_ps, d_ps, dist, neg_max = {}, {}, {}, {}
-        expo, expo_sum = {}, {}
+        expo, expo_sum, inv_sum = {}, {}, {}
         affinity, aff_flipped, aff_grouped, aff_codes, aff_scales = {}, {}, {}, {}, {}
         val_grouped, val_codes, val_scales = {}, {}, {}
         o_ps, result = {}, {}
@@ -181,15 +180,17 @@ def tile_vidsam_pa_t_kernel(
                     accum_out=expo_sum[b][:, i : i + 1],
                 )
 
+        def invert_sums(b):
+            inv_sum[b] = work.tile([P, Q_TILES], F32, name="inv_sum")
+            nc.vector.reciprocal(out=inv_sum[b][:], in_=expo_sum[b][:])
+
         def normalise(b):
-            inv_sum = work.tile([P, Q_TILES], F32)
-            nc.vector.reciprocal(out=inv_sum[:], in_=expo_sum[b][:])
             affinity[b] = work.tile([P, Q_TILES, N], BF16, name="affinity")
             for i in range(Q_TILES):
                 nc.gpsimd.tensor_scalar(
                     out=affinity[b][:, i, :],
                     in0=expo[b][:, i, :],
-                    scalar1=inv_sum[:, i : i + 1],
+                    scalar1=inv_sum[b][:, i : i + 1],
                     scalar2=0.0,
                     op0=ALU.mult,
                     op1=ALU.add,
@@ -240,8 +241,8 @@ def tile_vidsam_pa_t_kernel(
                 )
 
         def quantise_values(b):
-            val_codes[b] = work.tile([P, C], U32, align_bytes=64, name="val_codes", bufs=VAL_LEAD + 3)
-            val_scales[b] = work.tile([P, C], U8, align_bytes=64, name="val_scales", bufs=VAL_LEAD + 3)
+            val_codes[b] = work.tile([P, C], U32, align_bytes=64, name="val_codes", bufs=5)
+            val_scales[b] = work.tile([P, C], U8, align_bytes=64, name="val_scales", bufs=5)
             nc.vector.quantize_mx(
                 out=val_codes[b][:].bitcast(FP8X4), scales=val_scales[b][:], in_=val_grouped[b][:]
             )
@@ -261,12 +262,14 @@ def tile_vidsam_pa_t_kernel(
                         stop=True,
                     )
 
-        def copy_result(b):
+        def copy_result_vector(b):
             result[b] = work.tile([P, C_TILES * Q], F32, name="result", bufs=3)
-            nc.scalar.copy(out=result[b][:, 0 : 2 * Q], in_=o_ps[b, 0][:].rearrange("r t p -> r (t p)"))
             nc.vector.tensor_copy(
                 out=result[b][:, 2 * Q : 4 * Q], in_=o_ps[b, 1][:].rearrange("r t p -> r (t p)")
             )
+
+        def copy_result_scalar(b):
+            nc.scalar.copy(out=result[b][:, 0 : 2 * Q], in_=o_ps[b, 0][:].rearrange("r t p -> r (t p)"))
 
         def store_result(b):
             nc.scalar.dma_start(
@@ -277,38 +280,37 @@ def tile_vidsam_pa_t_kernel(
             return 0 <= b < B
 
         prepare_queries(0)
-        for step in range(-VAL_LEAD, B + 2):
-            nxt, new, mid, old, val = step + 1, step, step - 1, step - 2, step + VAL_LEAD
-            if live(old):
-                group_affinity(old)
-            if live(val):
-                transpose_values(val)
-            if live(new):
-                scale_distances(new, 0)
-            if live(mid):
-                normalise(mid)
-            if live(new):
-                scale_distances(new, 1)
-            if live(nxt) and nxt % 2 == 0:
-                spread_shrinkage(nxt)
-            if live(old):
-                quantise_affinity(old)
-                read_memory(old)
-            if live(new):
-                row_maximum(new)
-            if live(old):
-                copy_result(old)
-            if live(nxt + 1):
-                prepare_queries(nxt + 1)
-            if live(nxt):
-                distances(nxt)
-            if live(mid):
-                transpose_affinity(mid)
-            if live(new):
-                exponentials(new)
-            if live(old):
-                store_result(old)
-            if live(val):
-                quantise_values(val)
-            if live(nxt) and nxt % 2 == 0:
-                copy_shrinkage(nxt)
+        for step in range(-1, B + 3):
+            if live(step - 1):
+                exponentials(step - 1)
+            if live(step):
+                transpose_values(step)
+                scale_distances(step, 0)
+                scale_distances(step, 1)
+                row_maximum(step)
+            if live(step + 2):
+                prepare_queries(step + 2)
+            if live(step - 2):
+                transpose_affinity(step - 2)
+            if live(step - 3):
+                read_memory(step - 3)
+            if live(step - 1):
+                invert_sums(step - 1)
+                normalise(step - 1)
+            if live(step - 3):
+                copy_result_vector(step - 3)
+            if live(step - 2):
+                group_affinity(step - 2)
+            if live(step - 3):
+                copy_result_scalar(step - 3)
+                store_result(step - 3)
+            if live(step):
+                quantise_values(step)
+            if live(step + 1):
+                if (step + 1) % 2 == 0:
+                    spread_shrinkage(step + 1)
+                distances(step + 1)
+                if (step + 1) % 2 == 0:
+                    copy_shrinkage(step + 1)
+            if live(step - 2):
+                quantise_affinity(step - 2)

@@ -41,7 +41,7 @@ def tile_vidsam_pa_t_kernel(
     with ExitStack() as ctx:
         consts = ctx.enter_context(tc.tile_pool(name="consts", bufs=1))
         loads = ctx.enter_context(tc.tile_pool(name="loads", bufs=B))
-        work = ctx.enter_context(tc.tile_pool(name="work", bufs=2))
+        work = ctx.enter_context(tc.tile_pool(name="work", bufs=3))
         psum = ctx.enter_context(tc.psum_pool(name="psum", bufs=8))
         ctx.enter_context(tc.manual_schedule())
 
@@ -89,7 +89,7 @@ def tile_vidsam_pa_t_kernel(
 
         qs_m2, prod = {}, {}
         spread_ps, shrink = {}, {}
-        bsq_ps, d_ps, dist, neg_max = {}, {}, {}, {}
+        bsq_ps, d_ps, dist, dist_min, neg_max = {}, {}, {}, {}, {}
         expo, expo_sum, inv_sum = {}, {}, {}
         affinity, aff_flipped, aff_grouped, aff_codes, aff_scales = {}, {}, {}, {}, {}
         val_grouped, val_codes, val_scales = {}, {}, {}
@@ -114,7 +114,7 @@ def tile_vidsam_pa_t_kernel(
                     )
 
         def copy_shrinkage(b):
-            spread = work.tile([P, 2, N], BF16)
+            spread = work.tile([P, 2, N], BF16, bufs=2)
             nc.vector.tensor_copy(out=spread[:], in_=spread_ps[b][:])
             shrink[b] = spread[:, 0, :]
             shrink[b + 1] = spread[:, 1, :]
@@ -159,12 +159,14 @@ def tile_vidsam_pa_t_kernel(
                 op1=ALU.mult,
             )
 
-        def row_maximum(b):
-            dist_min = work.tile([P, Q_TILES], F32)
-            nc.vector.tensor_reduce(out=dist_min[:], in_=dist[b][:], axis=AXIS.X, op=ALU.min)
+        def row_minimum(b):
+            dist_min[b] = work.tile([P, Q_TILES], F32, name="dist_min")
+            nc.vector.tensor_reduce(out=dist_min[b][:], in_=dist[b][:], axis=AXIS.X, op=ALU.min)
+
+        def negated_maximum(b):
             neg_max[b] = work.tile([P, Q_TILES], F32, name="neg_max")
             nc.vector.tensor_scalar(
-                out=neg_max[b][:], in0=dist_min[:], scalar1=INV_SQRT_CK, scalar2=None, op0=ALU.mult
+                out=neg_max[b][:], in0=dist_min[b][:], scalar1=INV_SQRT_CK, scalar2=None, op0=ALU.mult
             )
 
         def exponentials(b):
@@ -185,7 +187,7 @@ def tile_vidsam_pa_t_kernel(
             nc.vector.reciprocal(out=inv_sum[b][:], in_=expo_sum[b][:])
 
         def normalise(b):
-            affinity[b] = work.tile([P, Q_TILES, N], BF16, name="affinity")
+            affinity[b] = work.tile([P, Q_TILES, N], BF16, name="affinity", bufs=2)
             for i in range(Q_TILES):
                 nc.gpsimd.tensor_scalar(
                     out=affinity[b][:, i, :],
@@ -209,7 +211,7 @@ def tile_vidsam_pa_t_kernel(
                         )
 
         def group_affinity(b):
-            aff_grouped[b] = work.tile([P, Q, PACK], BF16, align_bytes=64, name="aff_grouped")
+            aff_grouped[b] = work.tile([P, Q, PACK], BF16, align_bytes=64, name="aff_grouped", bufs=2)
             nc.scalar.copy(out=aff_grouped[b][:], in_=aff_flipped[b][:].rearrange("q k p -> q p k"))
 
         def quantise_affinity(b):
@@ -223,7 +225,7 @@ def tile_vidsam_pa_t_kernel(
 
         def transpose_values(b):
             val_words = val_sb[b][:].bitcast(F32)
-            val_grouped[b] = work.tile([P, C * PACK], BF16, align_bytes=64, name="val_grouped")
+            val_grouped[b] = work.tile([P, C * PACK], BF16, align_bytes=64, name="val_grouped", bufs=2)
             grouped_words = val_grouped[b][:].bitcast(F32)
             for h in range(2):
                 flipped = psum.tile([P, 2, 2 * P], F32, tag="bank")
@@ -263,7 +265,7 @@ def tile_vidsam_pa_t_kernel(
                     )
 
         def copy_result_vector(b):
-            result[b] = work.tile([P, C_TILES * Q], F32, name="result", bufs=3)
+            result[b] = work.tile([P, C_TILES * Q], F32, name="result", bufs=4)
             nc.vector.tensor_copy(
                 out=result[b][:, 2 * Q : 4 * Q], in_=o_ps[b, 1][:].rearrange("r t p -> r (t p)")
             )
@@ -280,37 +282,41 @@ def tile_vidsam_pa_t_kernel(
             return 0 <= b < B
 
         prepare_queries(0)
-        for step in range(-1, B + 3):
+        for step in range(-1, B + 5):
+            if live(step - 4):
+                read_memory(step - 4)
             if live(step - 1):
                 exponentials(step - 1)
+            if live(step - 5):
+                store_result(step - 5)
+            if live(step - 3):
+                group_affinity(step - 3)
             if live(step):
                 transpose_values(step)
                 scale_distances(step, 0)
                 scale_distances(step, 1)
-                row_maximum(step)
+            if live(step - 1):
+                quantise_values(step - 1)
+            if live(step):
+                row_minimum(step)
+            if live(step - 2):
+                normalise(step - 2)
             if live(step + 2):
                 prepare_queries(step + 2)
-            if live(step - 2):
-                transpose_affinity(step - 2)
-            if live(step - 3):
-                read_memory(step - 3)
+            if live(step - 4):
+                copy_result_vector(step - 4)
+                copy_result_scalar(step - 4)
+            if live(step):
+                negated_maximum(step)
             if live(step - 1):
                 invert_sums(step - 1)
-                normalise(step - 1)
-            if live(step - 3):
-                copy_result_vector(step - 3)
-            if live(step - 2):
-                group_affinity(step - 2)
-            if live(step - 3):
-                copy_result_scalar(step - 3)
-                store_result(step - 3)
-            if live(step):
-                quantise_values(step)
             if live(step + 1):
                 if (step + 1) % 2 == 0:
                     spread_shrinkage(step + 1)
                 distances(step + 1)
-                if (step + 1) % 2 == 0:
-                    copy_shrinkage(step + 1)
             if live(step - 2):
-                quantise_affinity(step - 2)
+                transpose_affinity(step - 2)
+            if live(step + 1) and (step + 1) % 2 == 0:
+                copy_shrinkage(step + 1)
+            if live(step - 3):
+                quantise_affinity(step - 3)

@@ -22,6 +22,7 @@ Q_TILES = Q // P
 C_TILES = C // P
 PACK = 4
 INV_SQRT_CK = 1.0 / math.sqrt(128.0)
+LOAD_AHEAD = 4
 
 FLOPS = B * (2 * 2 * P * N * Q + 2 * C * N * Q)
 
@@ -49,7 +50,8 @@ def tile_vidsam_pa_t_kernel(
         nc.vector.memset(ms_rows[:], 0.0)
         nc.sync.dma_start(out=ms_rows[0:B, :], in_=memory_shrinkage)
         qe_sb, ksq_sb, qs_sb, key_sb, qk_sb, val_sb = {}, {}, {}, {}, {}, {}
-        for b in range(B):
+
+        def load(b):
             qs_sb[b] = loads.tile([P, Q], BF16, name="qs")
             nc.sync.dma_start(out=qs_sb[b][:], in_=query_key_sel[b])
             qk_sb[b] = loads.tile([P, Q], BF16, name="qk")
@@ -65,6 +67,9 @@ def tile_vidsam_pa_t_kernel(
                 out=val_sb[b][:],
                 in_=memory_value[b].rearrange("(r t) n -> r (t n)", t=C_TILES),
             )
+
+        for b in range(LOAD_AHEAD):
+            load(b)
 
         ident_bf = consts.tile([P, P], BF16)
         make_identity(nc, ident_bf[:])
@@ -88,7 +93,7 @@ def tile_vidsam_pa_t_kernel(
         nc.vector.tensor_copy(out=ms_cols[:], in_=ms_cols_ps[:, :, 0:B])
 
         qs_m2, prod = {}, {}
-        spread_ps, shrink = {}, {}
+        shrink = consts.tile([P, B, N], BF16)
         bsq_ps, d_ps, dist, dist_min, neg_max = {}, {}, {}, {}, {}
         expo, expo_sum, inv_sum = {}, {}, {}
         affinity, aff_flipped, aff_grouped, aff_codes, aff_scales = {}, {}, {}, {}, {}
@@ -96,39 +101,25 @@ def tile_vidsam_pa_t_kernel(
         o_ps, result = {}, {}
 
         def prepare_queries(b):
-            prod[b] = work.tile([P, Q], F32, name="prod", bufs=3)
-            nc.gpsimd.tensor_tensor(out=prod[b][:], in0=qs_sb[b][:], in1=qk_sb[b][:], op=ALU.mult)
             qs_m2[b] = work.tile([P, Q], BF16, name="qs_m2", bufs=3)
             nc.gpsimd.tensor_scalar(
                 out=qs_m2[b][:], in0=qs_sb[b][:], scalar1=-2.0, scalar2=0.0, op0=ALU.mult, op1=ALU.add
             )
+            prod[b] = work.tile([P, Q], F32, name="prod", bufs=3)
+            nc.gpsimd.tensor_tensor(out=prod[b][:], in0=qs_sb[b][:], in1=qk_sb[b][:], op=ALU.mult)
 
         def spread_shrinkage(b):
-            spread_ps[b] = psum.tile([P, 2, N], BF16, tag="bank", name="spread_ps")
+            spread_ps = psum.tile([P, 2, N], BF16, tag="bank")
             for j in range(2):
                 for k in range(4):
                     nc.tensor.transpose(
-                        spread_ps[b][:, j, k * P : (k + 1) * P],
+                        spread_ps[:, j, k * P : (k + 1) * P],
                         ms_cols[:, k, b + j : b + j + 1].to_broadcast([P, P]),
                         ident_bf[:],
                     )
-
-        def copy_shrinkage(b):
-            spread = work.tile([P, 2, N], BF16, bufs=2)
-            nc.vector.tensor_copy(out=spread[:], in_=spread_ps[b][:])
-            shrink[b] = spread[:, 0, :]
-            shrink[b + 1] = spread[:, 1, :]
+            nc.scalar.copy(out=shrink[:, b : b + 2, :], in_=spread_ps[:])
 
         def distances(b):
-            bsq_ps[b] = psum.tile([P, Q_TILES, 2], F32, tag="bank", name="bsq_ps")
-            for i in range(Q_TILES):
-                nc.tensor.matmul(
-                    out=bsq_ps[b][:, i, :],
-                    lhsT=prod[b][:, i * P : (i + 1) * P],
-                    rhs=ones_f32[:],
-                    start=True,
-                    stop=True,
-                )
             for i in range(Q_TILES):
                 q_cols = slice(i * P, (i + 1) * P)
                 d_ps[b, i] = psum.tile([P, 2, N // 2], F32, tag="bank", name="d_ps")
@@ -146,6 +137,15 @@ def tile_vidsam_pa_t_kernel(
                     start=False,
                     stop=True,
                 )
+            bsq_ps[b] = psum.tile([P, Q_TILES, 2], F32, tag="bank", name="bsq_ps")
+            for i in range(Q_TILES):
+                nc.tensor.matmul(
+                    out=bsq_ps[b][:, i, :],
+                    lhsT=prod[b][:, i * P : (i + 1) * P],
+                    rhs=ones_f32[:],
+                    start=True,
+                    stop=True,
+                )
 
         def scale_distances(b, i):
             if i == 0:
@@ -154,14 +154,17 @@ def tile_vidsam_pa_t_kernel(
                 out=dist[b][:, i, :],
                 in0=d_ps[b, i][:].rearrange("p e w -> p (e w)"),
                 scalar=bsq_ps[b][:, i, 0:1],
-                in1=shrink[b],
+                in1=shrink[:, b, :],
                 op0=ALU.add,
                 op1=ALU.mult,
             )
 
-        def row_minimum(b):
-            dist_min[b] = work.tile([P, Q_TILES], F32, name="dist_min")
-            nc.vector.tensor_reduce(out=dist_min[b][:], in_=dist[b][:], axis=AXIS.X, op=ALU.min)
+        def row_minimum(b, i):
+            if i == 0:
+                dist_min[b] = work.tile([P, Q_TILES], F32, name="dist_min")
+            nc.vector.tensor_reduce(
+                out=dist_min[b][:, i : i + 1], in_=dist[b][:, i, :], axis=AXIS.X, op=ALU.min
+            )
 
         def negated_maximum(b):
             neg_max[b] = work.tile([P, Q_TILES], F32, name="neg_max")
@@ -274,7 +277,7 @@ def tile_vidsam_pa_t_kernel(
             nc.scalar.copy(out=result[b][:, 0 : 2 * Q], in_=o_ps[b, 0][:].rearrange("r t p -> r (t p)"))
 
         def store_result(b):
-            nc.scalar.dma_start(
+            nc.sync.dma_start(
                 out=out[b].rearrange("(r t) p -> r (t p)", t=C_TILES), in_=result[b][:]
             )
 
@@ -283,40 +286,44 @@ def tile_vidsam_pa_t_kernel(
 
         prepare_queries(0)
         for step in range(-1, B + 5):
-            if live(step - 4):
-                read_memory(step - 4)
-            if live(step - 1):
-                exponentials(step - 1)
             if live(step - 5):
                 store_result(step - 5)
+            if live(step + LOAD_AHEAD + 1):
+                load(step + LOAD_AHEAD + 1)
+            if live(step - 1):
+                exponentials(step - 1)
             if live(step - 3):
                 group_affinity(step - 3)
             if live(step):
                 transpose_values(step)
+            if live(step - 4):
+                read_memory(step - 4)
+            if live(step):
                 scale_distances(step, 0)
                 scale_distances(step, 1)
-            if live(step - 1):
-                quantise_values(step - 1)
-            if live(step):
-                row_minimum(step)
+                row_minimum(step, 0)
+                row_minimum(step, 1)
             if live(step - 2):
                 normalise(step - 2)
             if live(step + 2):
                 prepare_queries(step + 2)
             if live(step - 4):
                 copy_result_vector(step - 4)
-                copy_result_scalar(step - 4)
             if live(step):
                 negated_maximum(step)
             if live(step - 1):
-                invert_sums(step - 1)
-            if live(step + 1):
-                if (step + 1) % 2 == 0:
-                    spread_shrinkage(step + 1)
-                distances(step + 1)
-            if live(step - 2):
-                transpose_affinity(step - 2)
-            if live(step + 1) and (step + 1) % 2 == 0:
-                copy_shrinkage(step + 1)
+                quantise_values(step - 1)
             if live(step - 3):
                 quantise_affinity(step - 3)
+            if live(step - 1):
+                invert_sums(step - 1)
+            if live(4 * (step + 1)):
+                spread_shrinkage(4 * (step + 1))
+            if live(step - 4):
+                copy_result_scalar(step - 4)
+            if live(step + 1):
+                distances(step + 1)
+            if live(4 * (step + 1)):
+                spread_shrinkage(4 * (step + 1) + 2)
+            if live(step - 2):
+                transpose_affinity(step - 2)

@@ -246,8 +246,8 @@ def tile_vidsam_pa_t_kernel(
                 )
 
         def quantise_values(b):
-            val_codes[b] = work.tile([P, C], U32, align_bytes=64, name="val_codes", bufs=5)
-            val_scales[b] = work.tile([P, C], U8, align_bytes=64, name="val_scales", bufs=5)
+            val_codes[b] = work.tile([P, C], U32, align_bytes=64, name="val_codes")
+            val_scales[b] = work.tile([P, C], U8, align_bytes=64, name="val_scales")
             nc.vector.quantize_mx(
                 out=val_codes[b][:].bitcast(FP8X4), scales=val_scales[b][:], in_=val_grouped[b][:]
             )
@@ -268,7 +268,7 @@ def tile_vidsam_pa_t_kernel(
                     )
 
         def copy_result_vector(b):
-            result[b] = work.tile([P, C_TILES * Q], F32, name="result", bufs=4)
+            result[b] = work.tile([P, C_TILES * Q], F32, name="result")
             nc.vector.tensor_copy(
                 out=result[b][:, 2 * Q : 4 * Q], in_=o_ps[b, 1][:].rearrange("r t p -> r (t p)")
             )
@@ -276,26 +276,25 @@ def tile_vidsam_pa_t_kernel(
         def copy_result_scalar(b):
             nc.scalar.copy(out=result[b][:, 0 : 2 * Q], in_=o_ps[b, 0][:].rearrange("r t p -> r (t p)"))
 
-        def store_result(b):
+        def store_result(b, h):
+            half = slice(h * 2 * Q, (h + 1) * 2 * Q)
             nc.sync.dma_start(
-                out=out[b].rearrange("(r t) p -> r (t p)", t=C_TILES), in_=result[b][:]
+                out=out[b].rearrange("(r t) p -> r (t p)", t=C_TILES)[:, half], in_=result[b][:, half]
             )
 
         def live(b):
             return 0 <= b < B
 
         prepare_queries(0)
-        for step in range(-1, B + 5):
-            if live(step - 5):
-                store_result(step - 5)
+        for step in range(-1, B + 4):
             if live(step + LOAD_AHEAD + 1):
                 load(step + LOAD_AHEAD + 1)
             if live(step - 1):
                 exponentials(step - 1)
             if live(step - 3):
                 group_affinity(step - 3)
-            if live(step):
-                transpose_values(step)
+            if live(step - 2):
+                transpose_values(step - 2)
             if live(step - 4):
                 read_memory(step - 4)
             if live(step):
@@ -307,20 +306,22 @@ def tile_vidsam_pa_t_kernel(
                 normalise(step - 2)
             if live(step + 2):
                 prepare_queries(step + 2)
-            if live(step - 4):
-                copy_result_vector(step - 4)
+            if live(step - 3):
+                quantise_values(step - 3)
             if live(step):
                 negated_maximum(step)
-            if live(step - 1):
-                quantise_values(step - 1)
             if live(step - 3):
                 quantise_affinity(step - 3)
             if live(step - 1):
                 invert_sums(step - 1)
+            if live(step - 4):
+                copy_result_vector(step - 4)
+                store_result(step - 4, 1)
             if live(4 * (step + 1)):
                 spread_shrinkage(4 * (step + 1))
             if live(step - 4):
                 copy_result_scalar(step - 4)
+                store_result(step - 4, 0)
             if live(step + 1):
                 distances(step + 1)
             if live(4 * (step + 1)):

@@ -306,17 +306,16 @@ def tile_vidsam_pa_t_kernel(
                 normalise(step - 2)
             if live(step + 2):
                 prepare_queries(step + 2)
-            if live(step - 3):
-                quantise_values(step - 3)
-            if live(step):
-                negated_maximum(step)
-            if live(step - 3):
-                quantise_affinity(step - 3)
-            if live(step - 1):
-                invert_sums(step - 1)
             if live(step - 4):
                 copy_result_vector(step - 4)
                 store_result(step - 4, 1)
+            if live(step):
+                negated_maximum(step)
+            if live(step - 3):
+                quantise_values(step - 3)
+                quantise_affinity(step - 3)
+            if live(step - 1):
+                invert_sums(step - 1)
             if live(4 * (step + 1)):
                 spread_shrinkage(4 * (step + 1))
             if live(step - 4):

import math
from contextlib import ExitStack

import concourse.mybir as mybir
from concourse.masks import make_identity

F32 = mybir.dt.float32
BF16 = mybir.dt.bfloat16
U32 = mybir.dt.uint32
U8 = mybir.dt.uint8
FP8X4 = mybir.dt.float8_e4m3fn_x4
ALU = mybir.AluOpType
ACT = mybir.ActivationFunctionType
AXIS = mybir.AxisListType

P = 128
B = 16
N = 512
Q = 256
C = 512
Q_TILES = Q // P
C_TILES = C // P
PACK = 4
INV_SQRT_CK = 1.0 / math.sqrt(128.0)
LOAD_AHEAD = 4

FLOPS = B * (2 * 2 * P * N * Q + 2 * C * N * Q)


def tile_vidsam_pa_t_kernel(
    tc,
    memory_key,
    memory_key_sq,
    query_key,
    query_selection,
    query_key_sel,
    memory_shrinkage,
    memory_value,
    out,
):
    nc = tc.nc
    with ExitStack() as ctx:
        consts = ctx.enter_context(tc.tile_pool(name="consts", bufs=1))
        loads = ctx.enter_context(tc.tile_pool(name="loads", bufs=B))
        work = ctx.enter_context(tc.tile_pool(name="work", bufs=3))
        psum = ctx.enter_context(tc.psum_pool(name="psum", bufs=8))
        ctx.enter_context(tc.manual_schedule())

        ms_rows = consts.tile([P, N], BF16)
        nc.vector.memset(ms_rows[:], 0.0)
        nc.sync.dma_start(out=ms_rows[0:B, :], in_=memory_shrinkage)
        qe_sb, ksq_sb, qs_sb, key_sb, qk_sb, val_sb = {}, {}, {}, {}, {}, {}

        def load(b):
            qs_sb[b] = loads.tile([P, Q], BF16, name="qs")
            nc.sync.dma_start(out=qs_sb[b][:], in_=query_key_sel[b])
            qk_sb[b] = loads.tile([P, Q], BF16, name="qk")
            nc.sync.dma_start(out=qk_sb[b][:], in_=query_key[b])
            qe_sb[b] = loads.tile([P, Q], BF16, name="qe")
            nc.sync.dma_start(out=qe_sb[b][:], in_=query_selection[b])
            ksq_sb[b] = loads.tile([P, N], BF16, name="ksq")
            nc.sync.dma_start(out=ksq_sb[b][:], in_=memory_key_sq[b])
            key_sb[b] = loads.tile([P, N], BF16, name="key")
            nc.sync.dma_start(out=key_sb[b][:], in_=memory_key[b])
            val_sb[b] = loads.tile([P, C_TILES * N], BF16, name="val")
            nc.sync.dma_start(
                out=val_sb[b][:],
                in_=memory_value[b].rearrange("(r t) n -> r (t n)", t=C_TILES),
            )

        for b in range(LOAD_AHEAD):
            load(b)

        ident_bf = consts.tile([P, P], BF16)
        make_identity(nc, ident_bf[:])
        ident_f32 = consts.tile([P, P], F32)
        make_identity(nc, ident_f32[:])
        ones_f32 = consts.tile([P, 2], F32)
        nc.vector.memset(ones_f32[:], 1.0)
        warm = consts.tile([P, 1], F32)
        nc.scalar.activation(out=warm[:], in_=ones_f32[:, 0:1], func=ACT.Exp)

        ms_rows_ew = ms_rows[:].rearrange("r (w e) -> r e w", e=2)
        ms_cols_ps = psum.tile([P, 4, P], BF16, tag="bank")
        for e in range(2):
            for u in range(2):
                nc.tensor.transpose(
                    ms_cols_ps[:, 2 * e + u, :],
                    ms_rows_ew[:, e, u * P : (u + 1) * P],
                    ident_bf[:],
                )
        ms_cols = consts.tile([P, 4, B], BF16)
        nc.vector.tensor_copy(out=ms_cols[:], in_=ms_cols_ps[:, :, 0:B])

        qs_m2, prod = {}, {}
        shrink = consts.tile([P, B, N], BF16)
        bsq_ps, d_ps, dist, dist_min, neg_max = {}, {}, {}, {}, {}
        expo, expo_sum, inv_sum = {}, {}, {}
        affinity, aff_flipped, aff_grouped, aff_codes, aff_scales = {}, {}, {}, {}, {}
        val_grouped, val_codes, val_scales = {}, {}, {}
        o_ps, result = {}, {}

        def prepare_queries(b):
            qs_m2[b] = work.tile([P, Q], BF16, name="qs_m2", bufs=3)
            nc.gpsimd.tensor_scalar(
                out=qs_m2[b][:], in0=qs_sb[b][:], scalar1=-2.0, scalar2=0.0, op0=ALU.mult, op1=ALU.add
            )
            prod[b] = work.tile([P, Q], F32, name="prod", bufs=3)
            nc.gpsimd.tensor_tensor(out=prod[b][:], in0=qs_sb[b][:], in1=qk_sb[b][:], op=ALU.mult)

        def spread_shrinkage(b):
            spread_ps = psum.tile([P, 2, N], BF16, tag="bank")
            for j in range(2):
                for k in range(4):
                    nc.tensor.transpose(
                        spread_ps[:, j, k * P : (k + 1) * P],
                        ms_cols[:, k, b + j : b + j + 1].to_broadcast([P, P]),
                        ident_bf[:],
                    )
            nc.scalar.copy(out=shrink[:, b : b + 2, :], in_=spread_ps[:])

        def distances(b):
            for i in range(Q_TILES):
                q_cols = slice(i * P, (i + 1) * P)
                d_ps[b, i] = psum.tile([P, 2, N // 2], F32, tag="bank", name="d_ps")
                nc.tensor.matmul(
                    out=d_ps[b, i][:],
                    lhsT=qe_sb[b][:, q_cols],
                    rhs=ksq_sb[b][:].rearrange("c (w e) -> c e w", e=2),
                    start=True,
                    stop=False,
                )
                nc.tensor.matmul(
                    out=d_ps[b, i][:],
                    lhsT=qs_m2[b][:, q_cols],
                    rhs=key_sb[b][:].rearrange("c (w e) -> c e w", e=2),
                    start=False,
                    stop=True,
                )
            bsq_ps[b] = psum.tile([P, Q_TILES, 2], F32, tag="bank", name="bsq_ps")
            for i in range(Q_TILES):
                nc.tensor.matmul(
                    out=bsq_ps[b][:, i, :],
                    lhsT=prod[b][:, i * P : (i + 1) * P],
                    rhs=ones_f32[:],
                    start=True,
                    stop=True,
                )

        def scale_distances(b, i):
            if i == 0:
                dist[b] = work.tile([P, Q_TILES, N], F32, name="dist")
            nc.vector.scalar_tensor_tensor(
                out=dist[b][:, i, :],
                in0=d_ps[b, i][:].rearrange("p e w -> p (e w)"),
                scalar=bsq_ps[b][:, i, 0:1],
                in1=shrink[:, b, :],
                op0=ALU.add,
                op1=ALU.mult,
            )

        def row_minimum(b, i):
            if i == 0:
                dist_min[b] = work.tile([P, Q_TILES], F32, name="dist_min")
            nc.vector.tensor_reduce(
                out=dist_min[b][:, i : i + 1], in_=dist[b][:, i, :], axis=AXIS.X, op=ALU.min
            )

        def negated_maximum(b):
            neg_max[b] = work.tile([P, Q_TILES], F32, name="neg_max")
            nc.vector.tensor_scalar(
                out=neg_max[b][:], in0=dist_min[b][:], scalar1=INV_SQRT_CK, scalar2=None, op0=ALU.mult
            )

        def exponentials(b):
            expo[b] = work.tile([P, Q_TILES, N], F32, name="expo")
            expo_sum[b] = work.tile([P, Q_TILES], F32, name="expo_sum")
            for i in range(Q_TILES):
                nc.scalar.activation(
                    out=expo[b][:, i, :],
                    in_=dist[b][:, i, :],
                    func=ACT.Exp,
                    bias=neg_max[b][:, i : i + 1],
                    scale=-INV_SQRT_CK,
                    accum_out=expo_sum[b][:, i : i + 1],
                )

        def invert_sums(b):
            inv_sum[b] = work.tile([P, Q_TILES], F32, name="inv_sum")
            nc.vector.reciprocal(out=inv_sum[b][:], in_=expo_sum[b][:])

        def normalise(b):
            affinity[b] = work.tile([P, Q_TILES, N], BF16, name="affinity", bufs=2)
            for i in range(Q_TILES):
                nc.gpsimd.tensor_scalar(
                    out=affinity[b][:, i, :],
                    in0=expo[b][:, i, :],
                    scalar1=inv_sum[b][:, i : i + 1],
                    scalar2=0.0,
                    op0=ALU.mult,
                    op1=ALU.add,
                )

        def transpose_affinity(b):
            aff_flipped[b] = psum.tile([P, PACK, Q], BF16, tag="bank", name="aff_flipped")
            for i in range(Q_TILES):
                for e in range(2):
                    for u in range(2):
                        first = (2 * e + u) * P
                        nc.tensor.transpose(
                            aff_flipped[b][:, 2 * u + e, i * P : (i + 1) * P],
                            affinity[b][:, i, first : first + P],
                            ident_bf[:],
                        )

        def group_affinity(b):
            aff_grouped[b] = work.tile([P, Q, PACK], BF16, align_bytes=64, name="aff_grouped", bufs=2)
            nc.scalar.copy(out=aff_grouped[b][:], in_=aff_flipped[b][:].rearrange("q k p -> q p k"))

        def quantise_affinity(b):
            aff_codes[b] = work.tile([P, Q], U32, align_bytes=64, name="aff_codes")
            aff_scales[b] = work.tile([P, Q], U8, align_bytes=64, name="aff_scales")
            nc.vector.quantize_mx(
                out=aff_codes[b][:].bitcast(FP8X4),
                scales=aff_scales[b][:],
                in_=aff_grouped[b][:].rearrange("q p k -> q (p k)"),
            )

        def transpose_values(b):
            val_words = val_sb[b][:].bitcast(F32)
            val_grouped[b] = work.tile([P, C * PACK], BF16, align_bytes=64, name="val_grouped", bufs=2)
            grouped_words = val_grouped[b][:].bitcast(F32)
            for h in range(2):
                flipped = psum.tile([P, 2, 2 * P], F32, tag="bank")
                for tl in range(2):
                    for u in range(2):
                        first = (2 * h + tl) * (N // 2) + u * P
                        nc.tensor.transpose(
                            flipped[:, u, tl * P : (tl + 1) * P],
                            val_words[:, first : first + P],
                            ident_f32[:],
                        )
                nc.scalar.copy(
                    out=grouped_words[:, h * N : (h + 1) * N].rearrange("q (c u) -> q c u", u=2),
                    in_=flipped[:].rearrange("q u c -> q c u"),
                )

        def quantise_values(b):
            val_codes[b] = work.tile([P, C], U32, align_bytes=64, name="val_codes")
            val_scales[b] = work.tile([P, C], U8, align_bytes=64, name="val_scales")
            nc.vector.quantize_mx(
                out=val_codes[b][:].bitcast(FP8X4), scales=val_scales[b][:], in_=val_grouped[b][:]
            )

        def read_memory(b):
            for h in range(2):
                o_ps[b, h] = psum.tile([P, 2, Q], F32, tag="bank", name="o_ps")
                for tl in range(2):
                    c_cols = slice((2 * h + tl) * P, (2 * h + tl + 1) * P)
                    nc.tensor.matmul_mx(
                        out=o_ps[b, h][:, tl, :],
                        lhsT=val_codes[b][:, c_cols].bitcast(FP8X4),
                        lhsT_scale=val_scales[b][:, c_cols],
                        rhs=aff_codes[b][:].bitcast(FP8X4),
                        rhs_scale=aff_scales[b][:],
                        start=True,
                        stop=True,
                    )

        def copy_result_vector(b):
            result[b] = work.tile([P, C_TILES * Q], F32, name="result")
            nc.vector.tensor_copy(
                out=result[b][:, 2 * Q : 4 * Q], in_=o_ps[b, 1][:].rearrange("r t p -> r (t p)")
            )

        def copy_result_scalar(b):
            nc.scalar.copy(out=result[b][:, 0 : 2 * Q], in_=o_ps[b, 0][:].rearrange("r t p -> r (t p)"))

        def store_result(b, h):
            half = slice(h * 2 * Q, (h + 1) * 2 * Q)
            nc.sync.dma_start(
                out=out[b].rearrange("(r t) p -> r (t p)", t=C_TILES)[:, half], in_=result[b][:, half]
            )

        def live(b):
            return 0 <= b < B

        prepare_queries(0)
        for step in range(-1, B + 4):
            if live(step + LOAD_AHEAD + 1):
                load(step + LOAD_AHEAD + 1)
            if live(step - 1):
                exponentials(step - 1)
            if live(step - 3):
                group_affinity(step - 3)
            if live(step - 2):
                transpose_values(step - 2)
            if live(step - 4):
                read_memory(step - 4)
            if live(step):
                scale_distances(step, 0)
                scale_distances(step, 1)
                row_minimum(step, 0)
                row_minimum(step, 1)
            if live(step - 2):
                normalise(step - 2)
            if live(step + 2):
                prepare_queries(step + 2)
            if live(step - 4):
                copy_result_vector(step - 4)
                store_result(step - 4, 1)
            if live(step):
                negated_maximum(step)
            if live(step - 3):
                quantise_values(step - 3)
                quantise_affinity(step - 3)
            if live(step - 1):
                invert_sums(step - 1)
            if live(4 * (step + 1)):
                spread_shrinkage(4 * (step + 1))
            if live(step - 4):
                copy_result_scalar(step - 4)
                store_result(step - 4, 0)
            if live(step + 1):
                distances(step + 1)
            if live(4 * (step + 1)):
                spread_shrinkage(4 * (step + 1) + 2)
            if live(step - 2):
                transpose_affinity(step - 2)
